import numpy as np
import ml_dtypes

BF16 = ml_dtypes.bfloat16


def bf(x):
    return np.asarray(x, np.float32).astype(BF16)


def f32(x):
    return np.asarray(x, np.float32)


def f64(x):
    return np.asarray(x).astype(np.float64)


def striped(idx):
    return np.tile(idx.reshape(-1, 16).T, (8, 1))


C, S, N = 512, 1024, 1024


def setup_inputs():
    return {"labels": f32(np.random.uniform(0.0, 1.0, (C, S))), "lam": f32(np.random.uniform(0.1, 0.9, (1, N))), "dec": f32(np.random.uniform(0.2, 1.0, (1, N))), "offs": striped(np.random.permutation(S)[:N])}


def reference(labels, lam, dec, offs):
    idx = offs[:16].T.reshape(-1)
    y = f64(labels)
    l = f64(lam)
    d = f64(dec)
    mix = l * y + (1.0 - l) * y[:, idx]
    return d * mix + (1.0 - d) * y

@@ -1,0 +1,48 @@
+import concourse.mybir as mybir
+
+F32 = mybir.dt.float32
+U16 = mybir.dt.uint16
+MULT = mybir.AluOpType.mult
+ADD = mybir.AluOpType.add
+
+P = 128
+
+
+def tile_cutmix_kernel(tc, labels, lam, dec, offs, out):
+    nc = tc.nc
+    classes, samples = labels.shape
+    blocks = classes // P
+
+    with (
+        tc.tile_pool(name="held", bufs=1) as held,
+        tc.tile_pool(name="work", bufs=2) as work,
+    ):
+        offsets = held.tile([P, samples // 16], U16, name="offsets")
+        nc.sync.dma_start(offsets[:], offs)
+
+        lam_rows = held.tile([P, samples], F32, name="lam_rows")
+        dec_rows = held.tile([P, samples], F32, name="dec_rows")
+        nc.scalar.dma_start(lam_rows[:], lam[0, :].partition_broadcast(P))
+        nc.sync.dma_start(dec_rows[:], dec[0, :].partition_broadcast(P))
+
+        tables = []
+        for b in range(blocks):
+            table = held.tile([P, samples], F32, name=f"table{b}")
+            queue = nc.scalar if b % 2 == 0 else nc.sync
+            queue.dma_start(table[:], labels[b * P : (b + 1) * P, :])
+            tables.append(table)
+
+        share = held.tile([P, samples], F32, name="share")
+        keep = held.tile([P, samples], F32, name="keep")
+        nc.vector.tensor_scalar(share[:], lam_rows[:], -1.0, 1.0, MULT, ADD)
+        nc.vector.tensor_tensor(share[:], share[:], dec_rows[:], MULT)
+        nc.vector.tensor_scalar(keep[:], share[:], -1.0, 1.0, MULT, ADD)
+
+        for b in range(blocks):
+            partner = work.tile([P, samples], F32, name="partner")
+            nc.vector.tensor_tensor(partner[:], tables[b][:].indirect(offsets[:]), share[:], MULT)
+            own = work.tile([P, samples], F32, name="own")
+            nc.vector.tensor_tensor(own[:], tables[b][:], keep[:], MULT)
+            mixed = work.tile([P, samples], F32, name="mixed")
+            nc.vector.tensor_tensor(mixed[:], partner[:], own[:], ADD)
+            nc.sync.dma_start(out[b * P : (b + 1) * P, :], mixed[:])

@@ -1,48 +1,84 @@
 import concourse.mybir as mybir
+from concourse.masks import make_identity
 
 F32 = mybir.dt.float32
 U16 = mybir.dt.uint16
 MULT = mybir.AluOpType.mult
-ADD = mybir.AluOpType.add
+SUBTRACT = mybir.AluOpType.subtract
+IDENTITY = mybir.ActivationFunctionType.Identity
 
 P = 128
+BANK = 512
+PE_COLS = 512
 
 
 def tile_cutmix_kernel(tc, labels, lam, dec, offs, out):
     nc = tc.nc
     classes, samples = labels.shape
     blocks = classes // P
+    pieces = ((0, PE_COLS), (PE_COLS, samples))
 
     with (
         tc.tile_pool(name="held", bufs=1) as held,
-        tc.tile_pool(name="work", bufs=2) as work,
+        tc.tile_pool(name="work", bufs=4) as work,
+        tc.psum_pool(name="psum", bufs=2) as psum,
     ):
         offsets = held.tile([P, samples // 16], U16, name="offsets")
         nc.sync.dma_start(offsets[:], offs)
 
         lam_rows = held.tile([P, samples], F32, name="lam_rows")
         dec_rows = held.tile([P, samples], F32, name="dec_rows")
-        nc.scalar.dma_start(lam_rows[:], lam[0, :].partition_broadcast(P))
-        nc.sync.dma_start(dec_rows[:], dec[0, :].partition_broadcast(P))
+        tables = [held.tile([P, samples], F32, name=f"table{b}") for b in range(blocks)]
 
-        tables = []
-        for b in range(blocks):
-            table = held.tile([P, samples], F32, name=f"table{b}")
-            queue = nc.scalar if b % 2 == 0 else nc.sync
-            queue.dma_start(table[:], labels[b * P : (b + 1) * P, :])
-            tables.append(table)
+        def load_weights(lo, hi):
+            nc.sync.dma_start(lam_rows[:, lo:hi], lam[0, lo:hi].partition_broadcast(P))
+            nc.scalar.dma_start(dec_rows[:, lo:hi], dec[0, lo:hi].partition_broadcast(P))
 
-        share = held.tile([P, samples], F32, name="share")
+        def load_table(b, queue):
+            queue.dma_start(tables[b][:], labels[b * P : (b + 1) * P, :])
+
+        load_weights(0, PE_COLS)
+        load_table(0, nc.sync)
+        load_weights(PE_COLS, samples)
+        load_table(1, nc.scalar)
+        load_table(2, nc.sync)
+        load_table(3, nc.scalar)
+
+        identity = held.tile([P, P], F32, name="identity")
+        minus_identity = held.tile([P, P], F32, name="minus_identity")
+        make_identity(nc, identity[:])
+        nc.scalar.mul(minus_identity[:], identity[:], -1.0)
+
+        minus_share = held.tile([P, samples], F32, name="minus_share")
         keep = held.tile([P, samples], F32, name="keep")
-        nc.vector.tensor_scalar(share[:], lam_rows[:], -1.0, 1.0, MULT, ADD)
-        nc.vector.tensor_tensor(share[:], share[:], dec_rows[:], MULT)
-        nc.vector.tensor_scalar(keep[:], share[:], -1.0, 1.0, MULT, ADD)
+        for lo, hi in pieces:
+            nc.vector.scalar_tensor_tensor(
+                minus_share[:, lo:hi], lam_rows[:, lo:hi], 1.0, dec_rows[:, lo:hi], SUBTRACT, MULT
+            )
+            nc.scalar.activation(keep[:, lo:hi], minus_share[:, lo:hi], IDENTITY, bias=1.0, scale=1.0)
 
         for b in range(blocks):
-            partner = work.tile([P, samples], F32, name="partner")
-            nc.vector.tensor_tensor(partner[:], tables[b][:].indirect(offsets[:]), share[:], MULT)
+            rows = slice(b * P, (b + 1) * P)
             own = work.tile([P, samples], F32, name="own")
             nc.vector.tensor_tensor(own[:], tables[b][:], keep[:], MULT)
-            mixed = work.tile([P, samples], F32, name="mixed")
-            nc.vector.tensor_tensor(mixed[:], partner[:], own[:], ADD)
-            nc.sync.dma_start(out[b * P : (b + 1) * P, :], mixed[:])
+            partner = work.tile([P, samples], F32, name="partner")
+            for lo, hi in pieces:
+                nc.vector.tensor_tensor(
+                    partner[:, lo:hi],
+                    tables[b][:].indirect(offsets[:, lo // 16 : hi // 16]),
+                    minus_share[:, lo:hi],
+                    MULT,
+                )
+
+            mixed_pe = work.tile([P, PE_COLS], F32, name="mixed_pe")
+            for lo in range(0, PE_COLS, BANK):
+                hi = min(lo + BANK, PE_COLS)
+                summed = psum.tile([P, hi - lo], F32, name="summed")
+                nc.tensor.matmul(summed[:], identity[:], own[:, lo:hi], start=True, stop=False)
+                nc.tensor.matmul(summed[:], minus_identity[:], partner[:, lo:hi], start=False, stop=True)
+                nc.scalar.copy(mixed_pe[:, lo:hi], summed[:])
+            nc.sync.dma_start(out[rows, 0:PE_COLS], mixed_pe[:])
+
+            mixed_ve = work.tile([P, samples - PE_COLS], F32, name="mixed_ve")
+            nc.vector.tensor_tensor(mixed_ve[:], own[:, PE_COLS:], partner[:, PE_COLS:], SUBTRACT)
+            nc.sync.dma_start(out[rows, PE_COLS:], mixed_ve[:])

@@ -1,5 +1,4 @@
 import concourse.mybir as mybir
-from concourse.masks import make_identity
 
 F32 = mybir.dt.float32
 U16 = mybir.dt.uint16
@@ -9,76 +8,51 @@ IDENTITY = mybir.ActivationFunctionType.Identity
 
 P = 128
 BANK = 512
-PE_COLS = 512
 
 
 def tile_cutmix_kernel(tc, labels, lam, dec, offs, out):
     nc = tc.nc
     classes, samples = labels.shape
     blocks = classes // P
-    pieces = ((0, PE_COLS), (PE_COLS, samples))
 
     with (
         tc.tile_pool(name="held", bufs=1) as held,
-        tc.tile_pool(name="work", bufs=4) as work,
+        tc.tile_pool(name="work", bufs=2) as work,
         tc.psum_pool(name="psum", bufs=2) as psum,
     ):
         offsets = held.tile([P, samples // 16], U16, name="offsets")
         nc.sync.dma_start(offsets[:], offs)
 
-        lam_rows = held.tile([P, samples], F32, name="lam_rows")
-        dec_rows = held.tile([P, samples], F32, name="dec_rows")
-        tables = [held.tile([P, samples], F32, name=f"table{b}") for b in range(blocks)]
+        lam_row = held.tile([1, samples], F32, name="lam_row")
+        dec_row = held.tile([1, samples], F32, name="dec_row")
+        nc.sync.dma_start(lam_row[:], lam)
+        nc.scalar.dma_start(dec_row[:], dec)
 
-        def load_weights(lo, hi):
-            nc.sync.dma_start(lam_rows[:, lo:hi], lam[0, lo:hi].partition_broadcast(P))
-            nc.scalar.dma_start(dec_rows[:, lo:hi], dec[0, lo:hi].partition_broadcast(P))
+        tables = []
+        for b in range(blocks):
+            table = held.tile([P, samples], F32, name=f"table{b}")
+            queue = nc.sync if b % 2 == 0 else nc.scalar
+            queue.dma_start(table[:], labels[b * P : (b + 1) * P, :])
+            tables.append(table)
 
-        def load_table(b, queue):
-            queue.dma_start(tables[b][:], labels[b * P : (b + 1) * P, :])
-
-        load_weights(0, PE_COLS)
-        load_table(0, nc.sync)
-        load_weights(PE_COLS, samples)
-        load_table(1, nc.scalar)
-        load_table(2, nc.sync)
-        load_table(3, nc.scalar)
-
-        identity = held.tile([P, P], F32, name="identity")
-        minus_identity = held.tile([P, P], F32, name="minus_identity")
-        make_identity(nc, identity[:])
-        nc.scalar.mul(minus_identity[:], identity[:], -1.0)
-
+        ones = held.tile([1, P], F32, name="ones")
+        nc.gpsimd.memset(ones[:], 1.0)
+        minus_share_row = held.tile([1, samples], F32, name="minus_share_row")
+        nc.vector.scalar_tensor_tensor(minus_share_row[:], lam_row[:], 1.0, dec_row[:], SUBTRACT, MULT)
         minus_share = held.tile([P, samples], F32, name="minus_share")
         keep = held.tile([P, samples], F32, name="keep")
-        for lo, hi in pieces:
-            nc.vector.scalar_tensor_tensor(
-                minus_share[:, lo:hi], lam_rows[:, lo:hi], 1.0, dec_rows[:, lo:hi], SUBTRACT, MULT
-            )
-            nc.scalar.activation(keep[:, lo:hi], minus_share[:, lo:hi], IDENTITY, bias=1.0, scale=1.0)
+        for lo in range(0, samples, BANK):
+            hi = lo + BANK
+            spread = psum.tile([P, BANK], F32, name="spread")
+            nc.tensor.matmul(spread[:], ones[:], minus_share_row[:, lo:hi], start=True, stop=True)
+            nc.scalar.copy(minus_share[:, lo:hi], spread[:])
+            nc.scalar.activation(keep[:, lo:hi], spread[:], IDENTITY, bias=1.0, scale=1.0)
 
         for b in range(blocks):
-            rows = slice(b * P, (b + 1) * P)
+            partner = work.tile([P, samples], F32, name="partner")
+            nc.vector.tensor_tensor(partner[:], tables[b][:].indirect(offsets[:]), minus_share[:], MULT)
             own = work.tile([P, samples], F32, name="own")
             nc.vector.tensor_tensor(own[:], tables[b][:], keep[:], MULT)
-            partner = work.tile([P, samples], F32, name="partner")
-            for lo, hi in pieces:
-                nc.vector.tensor_tensor(
-                    partner[:, lo:hi],
-                    tables[b][:].indirect(offsets[:, lo // 16 : hi // 16]),
-                    minus_share[:, lo:hi],
-                    MULT,
-                )
-
-            mixed_pe = work.tile([P, PE_COLS], F32, name="mixed_pe")
-            for lo in range(0, PE_COLS, BANK):
-                hi = min(lo + BANK, PE_COLS)
-                summed = psum.tile([P, hi - lo], F32, name="summed")
-                nc.tensor.matmul(summed[:], identity[:], own[:, lo:hi], start=True, stop=False)
-                nc.tensor.matmul(summed[:], minus_identity[:], partner[:, lo:hi], start=False, stop=True)
-                nc.scalar.copy(mixed_pe[:, lo:hi], summed[:])
-            nc.sync.dma_start(out[rows, 0:PE_COLS], mixed_pe[:])
-
-            mixed_ve = work.tile([P, samples - PE_COLS], F32, name="mixed_ve")
-            nc.vector.tensor_tensor(mixed_ve[:], own[:, PE_COLS:], partner[:, PE_COLS:], SUBTRACT)
-            nc.sync.dma_start(out[rows, PE_COLS:], mixed_ve[:])
+            mixed = work.tile([P, samples], F32, name="mixed")
+            nc.vector.tensor_tensor(mixed[:], own[:], partner[:], SUBTRACT)
+            nc.sync.dma_start(out[b * P : (b + 1) * P, :], mixed[:])

@@ -3,11 +3,10 @@ import concourse.mybir as mybir
 F32 = mybir.dt.float32
 U16 = mybir.dt.uint16
 MULT = mybir.AluOpType.mult
-SUBTRACT = mybir.AluOpType.subtract
+ADD = mybir.AluOpType.add
 IDENTITY = mybir.ActivationFunctionType.Identity
 
 P = 128
-BANK = 512
 
 
 def tile_cutmix_kernel(tc, labels, lam, dec, offs, out):
@@ -18,41 +17,35 @@ def tile_cutmix_kernel(tc, labels, lam, dec, offs, out):
     with (
         tc.tile_pool(name="held", bufs=1) as held,
         tc.tile_pool(name="work", bufs=2) as work,
-        tc.psum_pool(name="psum", bufs=2) as psum,
     ):
         offsets = held.tile([P, samples // 16], U16, name="offsets")
         nc.sync.dma_start(offsets[:], offs)
 
-        lam_row = held.tile([1, samples], F32, name="lam_row")
-        dec_row = held.tile([1, samples], F32, name="dec_row")
-        nc.sync.dma_start(lam_row[:], lam)
-        nc.scalar.dma_start(dec_row[:], dec)
+        tables = [held.tile([P, samples], F32, name=f"table{b}") for b in range(blocks)]
+        lam_rows = held.tile([P, samples], F32, name="lam_rows")
+        dec_rows = held.tile([P, samples], F32, name="dec_rows")
+        nc.sync.dma_start(tables[0][:], labels[0 * P : 1 * P, :])
+        nc.scalar.dma_start(tables[1][:], labels[1 * P : 2 * P, :])
+        nc.sync.dma_start(tables[2][:], labels[2 * P : 3 * P, :])
+        nc.scalar.dma_start(tables[3][:], labels[3 * P : 4 * P, :])
+        nc.sync.dma_start(lam_rows[:], lam[0, :].partition_broadcast(P))
+        nc.scalar.dma_start(dec_rows[:], dec[0, :].partition_broadcast(P))
 
-        tables = []
+        aways = []
         for b in range(blocks):
-            table = held.tile([P, samples], F32, name=f"table{b}")
-            queue = nc.sync if b % 2 == 0 else nc.scalar
-            queue.dma_start(table[:], labels[b * P : (b + 1) * P, :])
-            tables.append(table)
+            minus_table = held.tile([P, samples], F32, name=f"minus_table{b}")
+            nc.scalar.mul(minus_table[:], tables[b][:], -1.0)
+            away = held.tile([P, samples], F32, name=f"away{b}")
+            nc.vector.tensor_tensor(away[:], tables[b][:].indirect(offsets[:]), minus_table[:], ADD)
+            aways.append(away)
 
-        ones = held.tile([1, P], F32, name="ones")
-        nc.gpsimd.memset(ones[:], 1.0)
-        minus_share_row = held.tile([1, samples], F32, name="minus_share_row")
-        nc.vector.scalar_tensor_tensor(minus_share_row[:], lam_row[:], 1.0, dec_row[:], SUBTRACT, MULT)
-        minus_share = held.tile([P, samples], F32, name="minus_share")
-        keep = held.tile([P, samples], F32, name="keep")
-        for lo in range(0, samples, BANK):
-            hi = lo + BANK
-            spread = psum.tile([P, BANK], F32, name="spread")
-            nc.tensor.matmul(spread[:], ones[:], minus_share_row[:, lo:hi], start=True, stop=True)
-            nc.scalar.copy(minus_share[:, lo:hi], spread[:])
-            nc.scalar.activation(keep[:, lo:hi], spread[:], IDENTITY, bias=1.0, scale=1.0)
+        share = held.tile([P, samples], F32, name="share")
+        nc.scalar.activation(share[:], lam_rows[:], IDENTITY, bias=1.0, scale=-1.0)
+        nc.vector.tensor_tensor(share[:], share[:], dec_rows[:], MULT)
 
         for b in range(blocks):
-            partner = work.tile([P, samples], F32, name="partner")
-            nc.vector.tensor_tensor(partner[:], tables[b][:].indirect(offsets[:]), minus_share[:], MULT)
-            own = work.tile([P, samples], F32, name="own")
-            nc.vector.tensor_tensor(own[:], tables[b][:], keep[:], MULT)
+            step = work.tile([P, samples], F32, name="step")
+            nc.vector.tensor_tensor(step[:], aways[b][:], share[:], MULT)
             mixed = work.tile([P, samples], F32, name="mixed")
-            nc.vector.tensor_tensor(mixed[:], own[:], partner[:], SUBTRACT)
+            nc.vector.tensor_tensor(mixed[:], step[:], tables[b][:], ADD)
             nc.sync.dma_start(out[b * P : (b + 1) * P, :], mixed[:])

@@ -1,4 +1,5 @@
 import concourse.mybir as mybir
+from concourse.masks import make_identity
 
 F32 = mybir.dt.float32
 U16 = mybir.dt.uint16
@@ -7,6 +8,7 @@ ADD = mybir.AluOpType.add
 IDENTITY = mybir.ActivationFunctionType.Identity
 
 P = 128
+BANK = 512
 
 
 def tile_cutmix_kernel(tc, labels, lam, dec, offs, out):
@@ -16,7 +18,8 @@ def tile_cutmix_kernel(tc, labels, lam, dec, offs, out):
 
     with (
         tc.tile_pool(name="held", bufs=1) as held,
-        tc.tile_pool(name="work", bufs=2) as work,
+        tc.tile_pool(name="work", bufs=4) as work,
+        tc.psum_pool(name="psum", bufs=1) as psum,
     ):
         offsets = held.tile([P, samples // 16], U16, name="offsets")
         nc.sync.dma_start(offsets[:], offs)
@@ -31,21 +34,36 @@ def tile_cutmix_kernel(tc, labels, lam, dec, offs, out):
         nc.sync.dma_start(lam_rows[:], lam[0, :].partition_broadcast(P))
         nc.scalar.dma_start(dec_rows[:], dec[0, :].partition_broadcast(P))
 
+        identity = held.tile([P, P], F32, name="identity")
+        make_identity(nc, identity[:])
+
         aways = []
+        sums = []
         for b in range(blocks):
             minus_table = held.tile([P, samples], F32, name=f"minus_table{b}")
             nc.scalar.mul(minus_table[:], tables[b][:], -1.0)
             away = held.tile([P, samples], F32, name=f"away{b}")
             nc.vector.tensor_tensor(away[:], tables[b][:].indirect(offsets[:]), minus_table[:], ADD)
             aways.append(away)
+            summed = psum.tile([P, BANK], F32, name=f"summed{b}")
+            nc.tensor.matmul(summed[:], identity[:], tables[b][:, 0:BANK], start=True, stop=False)
+            sums.append(summed)
 
         share = held.tile([P, samples], F32, name="share")
         nc.scalar.activation(share[:], lam_rows[:], IDENTITY, bias=1.0, scale=-1.0)
         nc.vector.tensor_tensor(share[:], share[:], dec_rows[:], MULT)
 
         for b in range(blocks):
+            rows = slice(b * P, (b + 1) * P)
             step = work.tile([P, samples], F32, name="step")
-            nc.vector.tensor_tensor(step[:], aways[b][:], share[:], MULT)
-            mixed = work.tile([P, samples], F32, name="mixed")
-            nc.vector.tensor_tensor(mixed[:], step[:], tables[b][:], ADD)
-            nc.sync.dma_start(out[b * P : (b + 1) * P, :], mixed[:])
+            nc.vector.tensor_tensor(step[:, 0:BANK], aways[b][:, 0:BANK], share[:, 0:BANK], MULT)
+            nc.vector.tensor_tensor(step[:, BANK:], aways[b][:, BANK:], share[:, BANK:], MULT)
+
+            nc.tensor.matmul(sums[b][:], identity[:], step[:, 0:BANK], start=False, stop=True)
+            mixed_pe = work.tile([P, BANK], F32, name="mixed_pe")
+            nc.scalar.copy(mixed_pe[:], sums[b][:])
+            nc.sync.dma_start(out[rows, 0:BANK], mixed_pe[:])
+
+            mixed_ve = work.tile([P, samples - BANK], F32, name="mixed_ve")
+            nc.vector.tensor_tensor(mixed_ve[:], step[:, BANK:], tables[b][:, BANK:], ADD)
+            nc.sync.dma_start(out[rows, BANK:], mixed_ve[:])

@@ -5,10 +5,12 @@ F32 = mybir.dt.float32
 U16 = mybir.dt.uint16
 MULT = mybir.AluOpType.mult
 ADD = mybir.AluOpType.add
-IDENTITY = mybir.ActivationFunctionType.Identity
+NOT_EQUAL = mybir.AluOpType.not_equal
 
 P = 128
 BANK = 512
+FIRST = 384
+ROWS = 8
 
 
 def tile_cutmix_kernel(tc, labels, lam, dec, offs, out):
@@ -18,52 +20,79 @@ def tile_cutmix_kernel(tc, labels, lam, dec, offs, out):
 
     with (
         tc.tile_pool(name="held", bufs=1) as held,
+        tc.tile_pool(name="turn", bufs=2) as turn,
         tc.tile_pool(name="work", bufs=4) as work,
         tc.psum_pool(name="psum", bufs=1) as psum,
     ):
         offsets = held.tile([P, samples // 16], U16, name="offsets")
         nc.sync.dma_start(offsets[:], offs)
 
-        tables = [held.tile([P, samples], F32, name=f"table{b}") for b in range(blocks)]
-        lam_rows = held.tile([P, samples], F32, name="lam_rows")
-        dec_rows = held.tile([P, samples], F32, name="dec_rows")
-        nc.sync.dma_start(tables[0][:], labels[0 * P : 1 * P, :])
-        nc.scalar.dma_start(tables[1][:], labels[1 * P : 2 * P, :])
-        nc.sync.dma_start(tables[2][:], labels[2 * P : 3 * P, :])
-        nc.scalar.dma_start(tables[3][:], labels[3 * P : 4 * P, :])
-        nc.sync.dma_start(lam_rows[:], lam[0, :].partition_broadcast(P))
-        nc.scalar.dma_start(dec_rows[:], dec[0, :].partition_broadcast(P))
+        lam_folded = held.tile([ROWS, P], F32, name="lam_folded")
+        dec_folded = held.tile([ROWS, P], F32, name="dec_folded")
+        nc.sync.dma_start(lam_folded[:], lam[0, :].rearrange("(r n) -> r n", r=ROWS))
+        nc.scalar.dma_start(dec_folded[:], dec[0, :].rearrange("(r n) -> r n", r=ROWS))
+
+        tables = []
+        for b in range(blocks):
+            table = held.tile([P, samples], F32, name=f"table{b}")
+            queue = nc.scalar if b % 2 == 0 else nc.sync
+            queue.dma_start(table[:], labels[b * P : (b + 1) * P, :])
+            tables.append(table)
 
         identity = held.tile([P, P], F32, name="identity")
         make_identity(nc, identity[:])
 
-        aways = []
-        sums = []
-        for b in range(blocks):
-            minus_table = held.tile([P, samples], F32, name=f"minus_table{b}")
-            nc.scalar.mul(minus_table[:], tables[b][:], -1.0)
-            away = held.tile([P, samples], F32, name=f"away{b}")
-            nc.vector.tensor_tensor(away[:], tables[b][:].indirect(offsets[:]), minus_table[:], ADD)
-            aways.append(away)
-            summed = psum.tile([P, BANK], F32, name=f"summed{b}")
-            nc.tensor.matmul(summed[:], identity[:], tables[b][:, 0:BANK], start=True, stop=False)
-            sums.append(summed)
+        share_folded = held.tile([ROWS, P], F32, name="share_folded")
+        nc.vector.tensor_scalar(share_folded[:], lam_folded[:], -1.0, 1.0, MULT, ADD)
+        nc.vector.tensor_tensor(share_folded[:], share_folded[:], dec_folded[:], MULT)
 
+        pick = held.tile([ROWS, ROWS * P], F32, name="pick")
+        nc.gpsimd.memset(pick[:], 0.0)
+        nc.gpsimd.affine_select(
+            out=pick[:],
+            in_=pick[:],
+            compare_op=NOT_EQUAL,
+            fill=1.0,
+            base=0,
+            pattern=[[-1, ROWS], [0, P]],
+            channel_multiplier=1,
+        )
         share = held.tile([P, samples], F32, name="share")
-        nc.scalar.activation(share[:], lam_rows[:], IDENTITY, bias=1.0, scale=-1.0)
-        nc.vector.tensor_tensor(share[:], share[:], dec_rows[:], MULT)
+        for lo in range(0, samples, BANK):
+            spread = psum.tile([P, BANK], F32, name=f"spread{lo}")
+            for r in range(lo // P, (lo + BANK) // P):
+                nc.tensor.matmul(
+                    spread[:, r * P - lo : (r + 1) * P - lo],
+                    pick[:, r * P : (r + 1) * P],
+                    share_folded[:],
+                    start=True,
+                    stop=True,
+                )
+            nc.scalar.copy(share[:, lo : lo + BANK], spread[:])
 
         for b in range(blocks):
             rows = slice(b * P, (b + 1) * P)
-            step = work.tile([P, samples], F32, name="step")
-            nc.vector.tensor_tensor(step[:, 0:BANK], aways[b][:, 0:BANK], share[:, 0:BANK], MULT)
-            nc.vector.tensor_tensor(step[:, BANK:], aways[b][:, BANK:], share[:, BANK:], MULT)
+            table = tables[b]
 
-            nc.tensor.matmul(sums[b][:], identity[:], step[:, 0:BANK], start=False, stop=True)
-            mixed_pe = work.tile([P, BANK], F32, name="mixed_pe")
-            nc.scalar.copy(mixed_pe[:], sums[b][:])
-            nc.sync.dma_start(out[rows, 0:BANK], mixed_pe[:])
+            minus_table = work.tile([P, samples], F32, name="minus_table")
+            away = turn.tile([P, samples], F32, name="away")
+            for lo, hi in ((0, FIRST), (FIRST, samples)):
+                nc.scalar.mul(minus_table[:, lo:hi], table[:, lo:hi], -1.0)
+                nc.vector.tensor_tensor(
+                    away[:, lo:hi], table[:].indirect(offsets[:, lo // 16 : hi // 16]), minus_table[:, lo:hi], ADD
+                )
 
-            mixed_ve = work.tile([P, samples - BANK], F32, name="mixed_ve")
-            nc.vector.tensor_tensor(mixed_ve[:], step[:, BANK:], tables[b][:, BANK:], ADD)
-            nc.sync.dma_start(out[rows, BANK:], mixed_ve[:])
+            step_first = work.tile([P, FIRST], F32, name="step_first")
+            nc.vector.tensor_tensor(step_first[:], away[:, 0:FIRST], share[:, 0:FIRST], MULT)
+            summed = psum.tile([P, FIRST], F32, name=f"summed{b}")
+            nc.tensor.matmul(summed[:], identity[:], table[:, 0:FIRST], start=True, stop=False)
+            nc.tensor.matmul(summed[:], identity[:], step_first[:], start=False, stop=True)
+            mixed_first = work.tile([P, FIRST], F32, name="mixed_first")
+            nc.scalar.copy(mixed_first[:], summed[:])
+            nc.sync.dma_start(out[rows, 0:FIRST], mixed_first[:])
+
+            step_second = work.tile([P, samples - FIRST], F32, name="step_second")
+            nc.vector.tensor_tensor(step_second[:], away[:, FIRST:], share[:, FIRST:], MULT)
+            mixed_second = work.tile([P, samples - FIRST], F32, name="mixed_second")
+            nc.vector.tensor_tensor(mixed_second[:], step_second[:], table[:, FIRST:], ADD)
+            nc.sync.dma_start(out[rows, FIRST:], mixed_second[:])

@@ -20,7 +20,6 @@ def tile_cutmix_kernel(tc, labels, lam, dec, offs, out):
 
     with (
         tc.tile_pool(name="held", bufs=1) as held,
-        tc.tile_pool(name="turn", bufs=2) as turn,
         tc.tile_pool(name="work", bufs=4) as work,
         tc.psum_pool(name="psum", bufs=1) as psum,
     ):
@@ -75,7 +74,7 @@ def tile_cutmix_kernel(tc, labels, lam, dec, offs, out):
             table = tables[b]
 
             minus_table = work.tile([P, samples], F32, name="minus_table")
-            away = turn.tile([P, samples], F32, name="away")
+            away = work.tile([P, samples], F32, name="away")
             for lo, hi in ((0, FIRST), (FIRST, samples)):
                 nc.scalar.mul(minus_table[:, lo:hi], table[:, lo:hi], -1.0)
                 nc.vector.tensor_tensor(

@@ -28,14 +28,13 @@ def tile_cutmix_kernel(tc, labels, lam, dec, offs, out):
 
         lam_folded = held.tile([ROWS, P], F32, name="lam_folded")
         dec_folded = held.tile([ROWS, P], F32, name="dec_folded")
-        nc.sync.dma_start(lam_folded[:], lam[0, :].rearrange("(r n) -> r n", r=ROWS))
+        nc.scalar.dma_start(lam_folded[:], lam[0, :].rearrange("(r n) -> r n", r=ROWS))
         nc.scalar.dma_start(dec_folded[:], dec[0, :].rearrange("(r n) -> r n", r=ROWS))
 
         tables = []
         for b in range(blocks):
             table = held.tile([P, samples], F32, name=f"table{b}")
-            queue = nc.scalar if b % 2 == 0 else nc.sync
-            queue.dma_start(table[:], labels[b * P : (b + 1) * P, :])
+            nc.sync.dma_start(table[:], labels[b * P : (b + 1) * P, :])
             tables.append(table)
 
         identity = held.tile([P, P], F32, name="identity")

@@ -5,12 +5,11 @@ F32 = mybir.dt.float32
 U16 = mybir.dt.uint16
 MULT = mybir.AluOpType.mult
 ADD = mybir.AluOpType.add
-NOT_EQUAL = mybir.AluOpType.not_equal
 
 P = 128
 BANK = 512
-FIRST = 384
 ROWS = 8
+ROAD = (1024, 1024, 512, 256)
 
 
 def tile_cutmix_kernel(tc, labels, lam, dec, offs, out):
@@ -21,6 +20,7 @@ def tile_cutmix_kernel(tc, labels, lam, dec, offs, out):
     with (
         tc.tile_pool(name="held", bufs=1) as held,
         tc.tile_pool(name="work", bufs=4) as work,
+        tc.tile_pool(name="ahead", bufs=3) as ahead,
         tc.psum_pool(name="psum", bufs=1) as psum,
     ):
         offsets = held.tile([P, samples // 16], U16, name="offsets")
@@ -34,63 +34,56 @@ def tile_cutmix_kernel(tc, labels, lam, dec, offs, out):
         tables = []
         for b in range(blocks):
             table = held.tile([P, samples], F32, name=f"table{b}")
-            nc.sync.dma_start(table[:], labels[b * P : (b + 1) * P, :])
+            width = samples // 2 if b == 0 else samples
+            for lo in range(0, samples, width):
+                nc.sync.dma_start(table[:, lo : lo + width], labels[b * P : (b + 1) * P, lo : lo + width])
             tables.append(table)
-
-        identity = held.tile([P, P], F32, name="identity")
-        make_identity(nc, identity[:])
 
         share_folded = held.tile([ROWS, P], F32, name="share_folded")
         nc.vector.tensor_scalar(share_folded[:], lam_folded[:], -1.0, 1.0, MULT, ADD)
         nc.vector.tensor_tensor(share_folded[:], share_folded[:], dec_folded[:], MULT)
 
-        pick = held.tile([ROWS, ROWS * P], F32, name="pick")
-        nc.gpsimd.memset(pick[:], 0.0)
-        nc.gpsimd.affine_select(
-            out=pick[:],
-            in_=pick[:],
-            compare_op=NOT_EQUAL,
-            fill=1.0,
-            base=0,
-            pattern=[[-1, ROWS], [0, P]],
-            channel_multiplier=1,
-        )
+        nc.scalar.dma_start(out[0, :].rearrange("(r n) -> r n", r=ROWS), share_folded[:])
         share = held.tile([P, samples], F32, name="share")
-        for lo in range(0, samples, BANK):
-            spread = psum.tile([P, BANK], F32, name=f"spread{lo}")
-            for r in range(lo // P, (lo + BANK) // P):
-                nc.tensor.matmul(
-                    spread[:, r * P - lo : (r + 1) * P - lo],
-                    pick[:, r * P : (r + 1) * P],
-                    share_folded[:],
-                    start=True,
-                    stop=True,
-                )
-            nc.scalar.copy(share[:, lo : lo + BANK], spread[:])
+        nc.sync.dma_start(share[:], out[0, :].partition_broadcast(P))
+
+        identity = held.tile([P, P], F32, name="identity")
+        make_identity(nc, identity[:])
+        sums = []
+        for b in range(blocks):
+            banks = []
+            for lo in range(0, ROAD[b], BANK):
+                hi = min(lo + BANK, ROAD[b])
+                summed = psum.tile([P, hi - lo], F32, name=f"summed{b}_{lo}")
+                nc.tensor.matmul(summed[:], identity[:], tables[b][:, lo:hi], start=True, stop=False)
+                banks.append((lo, hi, summed))
+            sums.append(banks)
 
         for b in range(blocks):
             rows = slice(b * P, (b + 1) * P)
             table = tables[b]
 
             minus_table = work.tile([P, samples], F32, name="minus_table")
-            away = work.tile([P, samples], F32, name="away")
-            for lo, hi in ((0, FIRST), (FIRST, samples)):
+            away = ahead.tile([P, samples], F32, name="away")
+            width = samples // 2 if b == 0 else samples
+            for lo in range(0, samples, width):
+                hi = lo + width
                 nc.scalar.mul(minus_table[:, lo:hi], table[:, lo:hi], -1.0)
                 nc.vector.tensor_tensor(
                     away[:, lo:hi], table[:].indirect(offsets[:, lo // 16 : hi // 16]), minus_table[:, lo:hi], ADD
                 )
 
-            step_first = work.tile([P, FIRST], F32, name="step_first")
-            nc.vector.tensor_tensor(step_first[:], away[:, 0:FIRST], share[:, 0:FIRST], MULT)
-            summed = psum.tile([P, FIRST], F32, name=f"summed{b}")
-            nc.tensor.matmul(summed[:], identity[:], table[:, 0:FIRST], start=True, stop=False)
-            nc.tensor.matmul(summed[:], identity[:], step_first[:], start=False, stop=True)
-            mixed_first = work.tile([P, FIRST], F32, name="mixed_first")
-            nc.scalar.copy(mixed_first[:], summed[:])
-            nc.sync.dma_start(out[rows, 0:FIRST], mixed_first[:])
+            step = work.tile([P, samples], F32, name="step")
+            mixed = work.tile([P, samples], F32, name="mixed")
 
-            step_second = work.tile([P, samples - FIRST], F32, name="step_second")
-            nc.vector.tensor_tensor(step_second[:], away[:, FIRST:], share[:, FIRST:], MULT)
-            mixed_second = work.tile([P, samples - FIRST], F32, name="mixed_second")
-            nc.vector.tensor_tensor(mixed_second[:], step_second[:], table[:, FIRST:], ADD)
-            nc.sync.dma_start(out[rows, FIRST:], mixed_second[:])
+            for lo, hi, summed in sums[b]:
+                nc.vector.tensor_tensor(step[:, lo:hi], away[:, lo:hi], share[:, lo:hi], MULT)
+                nc.tensor.matmul(summed[:], identity[:], step[:, lo:hi], start=False, stop=True)
+                nc.scalar.copy(mixed[:, lo:hi], summed[:])
+                nc.sync.dma_start(out[rows, lo:hi], mixed[:, lo:hi])
+
+            for lo in range(ROAD[b], samples, BANK):
+                hi = min(lo + BANK, samples)
+                nc.vector.tensor_tensor(step[:, lo:hi], away[:, lo:hi], share[:, lo:hi], MULT)
+                nc.vector.tensor_tensor(mixed[:, lo:hi], step[:, lo:hi], table[:, lo:hi], ADD)
+                nc.sync.dma_start(out[rows, lo:hi], mixed[:, lo:hi])

@@ -9,7 +9,7 @@ ADD = mybir.AluOpType.add
 P = 128
 BANK = 512
 ROWS = 8
-ROAD = (1024, 1024, 512, 256)
+ROAD = (1024, 1024, 768, 256)
 
 
 def tile_cutmix_kernel(tc, labels, lam, dec, offs, out):
@@ -80,7 +80,7 @@ def tile_cutmix_kernel(tc, labels, lam, dec, offs, out):
                 nc.vector.tensor_tensor(step[:, lo:hi], away[:, lo:hi], share[:, lo:hi], MULT)
                 nc.tensor.matmul(summed[:], identity[:], step[:, lo:hi], start=False, stop=True)
                 nc.scalar.copy(mixed[:, lo:hi], summed[:])
-                nc.sync.dma_start(out[rows, lo:hi], mixed[:, lo:hi])
+                nc.scalar.dma_start(out[rows, lo:hi], mixed[:, lo:hi])
 
             for lo in range(ROAD[b], samples, BANK):
                 hi = min(lo + BANK, samples)

@@ -9,7 +9,7 @@ ADD = mybir.AluOpType.add
 P = 128
 BANK = 512
 ROWS = 8
-ROAD = (1024, 1024, 768, 256)
+ROAD = (1024, 1024, 1024, 256)
 
 
 def tile_cutmix_kernel(tc, labels, lam, dec, offs, out):

@@ -8,28 +8,27 @@ ADD = mybir.AluOpType.add
 
 P = 128
 BANK = 512
-ROWS = 8
-ROAD = (1024, 1024, 1024, 256)
 
 
 def tile_cutmix_kernel(tc, labels, lam, dec, offs, out):
     nc = tc.nc
     classes, samples = labels.shape
     blocks = classes // P
+    chunks = samples // P
 
     with (
         tc.tile_pool(name="held", bufs=1) as held,
         tc.tile_pool(name="work", bufs=4) as work,
-        tc.tile_pool(name="ahead", bufs=3) as ahead,
-        tc.psum_pool(name="psum", bufs=1) as psum,
+        tc.psum_pool(name="early", bufs=1) as early,
+        tc.psum_pool(name="turn", bufs=2) as turn,
     ):
         offsets = held.tile([P, samples // 16], U16, name="offsets")
         nc.sync.dma_start(offsets[:], offs)
 
-        lam_folded = held.tile([ROWS, P], F32, name="lam_folded")
-        dec_folded = held.tile([ROWS, P], F32, name="dec_folded")
-        nc.scalar.dma_start(lam_folded[:], lam[0, :].rearrange("(r n) -> r n", r=ROWS))
-        nc.scalar.dma_start(dec_folded[:], dec[0, :].rearrange("(r n) -> r n", r=ROWS))
+        lam_folded = held.tile([chunks, P], F32, name="lam_folded")
+        dec_folded = held.tile([chunks, P], F32, name="dec_folded")
+        nc.sync.dma_start(lam_folded[:], lam[0, :].rearrange("(r n) -> r n", r=chunks))
+        nc.sync.dma_start(dec_folded[:], dec[0, :].rearrange("(r n) -> r n", r=chunks))
 
         tables = []
         for b in range(blocks):
@@ -39,51 +38,73 @@ def tile_cutmix_kernel(tc, labels, lam, dec, offs, out):
                 nc.sync.dma_start(table[:, lo : lo + width], labels[b * P : (b + 1) * P, lo : lo + width])
             tables.append(table)
 
-        share_folded = held.tile([ROWS, P], F32, name="share_folded")
-        nc.vector.tensor_scalar(share_folded[:], lam_folded[:], -1.0, 1.0, MULT, ADD)
-        nc.vector.tensor_tensor(share_folded[:], share_folded[:], dec_folded[:], MULT)
-
-        nc.scalar.dma_start(out[0, :].rearrange("(r n) -> r n", r=ROWS), share_folded[:])
-        share = held.tile([P, samples], F32, name="share")
-        nc.sync.dma_start(share[:], out[0, :].partition_broadcast(P))
-
         identity = held.tile([P, P], F32, name="identity")
         make_identity(nc, identity[:])
-        sums = []
-        for b in range(blocks):
-            banks = []
-            for lo in range(0, ROAD[b], BANK):
-                hi = min(lo + BANK, ROAD[b])
-                summed = psum.tile([P, hi - lo], F32, name=f"summed{b}_{lo}")
-                nc.tensor.matmul(summed[:], identity[:], tables[b][:, lo:hi], start=True, stop=False)
-                banks.append((lo, hi, summed))
-            sums.append(banks)
 
+        share_folded = held.tile([P, P], F32, name="share_folded")
+        nc.gpsimd.memset(share_folded[:], 0.0)
+        nc.vector.tensor_scalar(share_folded[:chunks, :], lam_folded[:], -1.0, 1.0, MULT, ADD)
+        nc.vector.tensor_tensor(share_folded[:chunks, :], share_folded[:chunks, :], dec_folded[:], MULT)
+        share_flipped = turn.tile([P, BANK], F32, name="flipped")
+        nc.tensor.transpose(share_flipped[:, :P], share_folded[:], identity[:])
+        share_column = held.tile([P, chunks], F32, name="share_column")
+        nc.scalar.copy(share_column[:], share_flipped[:, :chunks])
+
+        with_labels = []
+        for b in range(blocks):
+            bank = early.tile([P, BANK], F32, name=f"with_labels{b}")
+            nc.tensor.matmul(bank[:], identity[:], tables[b][:, :BANK], start=True, stop=False)
+            with_labels.append(bank)
+
+        def negate(b):
+            minus_table = work.tile([P, samples], F32, name="minus_table")
+            width = samples // 2 if b == 0 else samples
+            for lo in range(0, samples, width):
+                nc.scalar.mul(minus_table[:, lo : lo + width], tables[b][:, lo : lo + width], -1.0)
+            return minus_table
+
+        minus_ahead = negate(0)
         for b in range(blocks):
             rows = slice(b * P, (b + 1) * P)
             table = tables[b]
+            minus_table = minus_ahead
+            if b + 1 < blocks:
+                minus_ahead = negate(b + 1)
 
-            minus_table = work.tile([P, samples], F32, name="minus_table")
-            away = ahead.tile([P, samples], F32, name="away")
-            width = samples // 2 if b == 0 else samples
+            away = work.tile([P, samples], F32, name="away")
+            width = samples // 2 if b in (0, blocks - 1) else samples
             for lo in range(0, samples, width):
                 hi = lo + width
-                nc.scalar.mul(minus_table[:, lo:hi], table[:, lo:hi], -1.0)
                 nc.vector.tensor_tensor(
                     away[:, lo:hi], table[:].indirect(offsets[:, lo // 16 : hi // 16]), minus_table[:, lo:hi], ADD
                 )
 
-            step = work.tile([P, samples], F32, name="step")
+            step_flipped = work.tile([P, samples], F32, name="step_flipped")
             mixed = work.tile([P, samples], F32, name="mixed")
-
-            for lo, hi, summed in sums[b]:
-                nc.vector.tensor_tensor(step[:, lo:hi], away[:, lo:hi], share[:, lo:hi], MULT)
-                nc.tensor.matmul(summed[:], identity[:], step[:, lo:hi], start=False, stop=True)
-                nc.scalar.copy(mixed[:, lo:hi], summed[:])
-                nc.scalar.dma_start(out[rows, lo:hi], mixed[:, lo:hi])
-
-            for lo in range(ROAD[b], samples, BANK):
-                hi = min(lo + BANK, samples)
-                nc.vector.tensor_tensor(step[:, lo:hi], away[:, lo:hi], share[:, lo:hi], MULT)
-                nc.vector.tensor_tensor(mixed[:, lo:hi], step[:, lo:hi], table[:, lo:hi], ADD)
-                nc.sync.dma_start(out[rows, lo:hi], mixed[:, lo:hi])
+            for lo in range(0, samples, BANK):
+                hi = lo + BANK
+                flipped = turn.tile([P, BANK], F32, name="flipped")
+                for at in range(0, BANK, P):
+                    nc.tensor.transpose(flipped[:, at : at + P], away[:, lo + at : lo + at + P], identity[:])
+                for at in range(0, BANK, P):
+                    r = (lo + at) // P
+                    nc.scalar.mul(step_flipped[:, lo + at : lo + at + P], flipped[:, at : at + P], share_column[:, r : r + 1])
+                if lo == 0:
+                    summed = with_labels[b]
+                else:
+                    summed = turn.tile([P, BANK], F32, name="step")
+                for at in range(0, BANK, P):
+                    nc.tensor.matmul(
+                        summed[:, at : at + P],
+                        step_flipped[:, lo + at : lo + at + P],
+                        identity[:],
+                        is_transpose=True,
+                        start=(lo > 0 and at == 0),
+                        stop=(at == BANK - P),
+                    )
+                if lo == 0:
+                    nc.scalar.copy(mixed[:, lo:hi], summed[:])
+                    nc.sync.dma_start(out[rows, lo:hi], mixed[:, lo:hi])
+                else:
+                    nc.vector.tensor_tensor(mixed[:, lo:hi], summed[:], table[:, lo:hi], ADD)
+                    nc.sync.dma_start(out[rows, lo:hi], mixed[:, lo:hi])

@@ -21,14 +21,15 @@ def tile_cutmix_kernel(tc, labels, lam, dec, offs, out):
         tc.tile_pool(name="work", bufs=4) as work,
         tc.psum_pool(name="early", bufs=1) as early,
         tc.psum_pool(name="turn", bufs=2) as turn,
+        tc.psum_pool(name="wait", bufs=4) as wait,
     ):
         offsets = held.tile([P, samples // 16], U16, name="offsets")
         nc.sync.dma_start(offsets[:], offs)
 
         lam_folded = held.tile([chunks, P], F32, name="lam_folded")
         dec_folded = held.tile([chunks, P], F32, name="dec_folded")
-        nc.sync.dma_start(lam_folded[:], lam[0, :].rearrange("(r n) -> r n", r=chunks))
-        nc.sync.dma_start(dec_folded[:], dec[0, :].rearrange("(r n) -> r n", r=chunks))
+        nc.scalar.dma_start(lam_folded[:], lam[0, :].rearrange("(r n) -> r n", r=chunks))
+        nc.scalar.dma_start(dec_folded[:], dec[0, :].rearrange("(r n) -> r n", r=chunks))
 
         tables = []
         for b in range(blocks):
@@ -50,11 +51,10 @@ def tile_cutmix_kernel(tc, labels, lam, dec, offs, out):
         share_column = held.tile([P, chunks], F32, name="share_column")
         nc.scalar.copy(share_column[:], share_flipped[:, :chunks])
 
-        with_labels = []
-        for b in range(blocks):
-            bank = early.tile([P, BANK], F32, name=f"with_labels{b}")
-            nc.tensor.matmul(bank[:], identity[:], tables[b][:, :BANK], start=True, stop=False)
-            with_labels.append(bank)
+        with_labels = {}
+        for b in range(blocks // 2):
+            with_labels[b] = early.tile([P, BANK], F32, name=f"with_labels{b}")
+            nc.tensor.matmul(with_labels[b][:], identity[:], tables[b][:, :BANK], start=True, stop=False)
 
         def negate(b):
             minus_table = work.tile([P, samples], F32, name="minus_table")
@@ -89,20 +89,21 @@ def tile_cutmix_kernel(tc, labels, lam, dec, offs, out):
                 for at in range(0, BANK, P):
                     r = (lo + at) // P
                     nc.scalar.mul(step_flipped[:, lo + at : lo + at + P], flipped[:, at : at + P], share_column[:, r : r + 1])
-                if lo == 0:
+                on_labels = lo == 0 and b in with_labels
+                if on_labels:
                     summed = with_labels[b]
                 else:
-                    summed = turn.tile([P, BANK], F32, name="step")
+                    summed = wait.tile([P, BANK], F32, name="step")
                 for at in range(0, BANK, P):
                     nc.tensor.matmul(
                         summed[:, at : at + P],
                         step_flipped[:, lo + at : lo + at + P],
                         identity[:],
                         is_transpose=True,
-                        start=(lo > 0 and at == 0),
+                        start=(at == 0 and not on_labels),
                         stop=(at == BANK - P),
                     )
-                if lo == 0:
+                if on_labels:
                     nc.scalar.copy(mixed[:, lo:hi], summed[:])
                     nc.sync.dma_start(out[rows, lo:hi], mixed[:, lo:hi])
                 else:

@@ -28,8 +28,8 @@ def tile_cutmix_kernel(tc, labels, lam, dec, offs, out):
 
         lam_folded = held.tile([chunks, P], F32, name="lam_folded")
         dec_folded = held.tile([chunks, P], F32, name="dec_folded")
-        nc.scalar.dma_start(lam_folded[:], lam[0, :].rearrange("(r n) -> r n", r=chunks))
-        nc.scalar.dma_start(dec_folded[:], dec[0, :].rearrange("(r n) -> r n", r=chunks))
+        nc.sync.dma_start(lam_folded[:], lam[0, :].rearrange("(r n) -> r n", r=chunks))
+        nc.sync.dma_start(dec_folded[:], dec[0, :].rearrange("(r n) -> r n", r=chunks))
 
         tables = []
         for b in range(blocks):

@@ -52,9 +52,9 @@ def tile_cutmix_kernel(tc, labels, lam, dec, offs, out):
         nc.scalar.copy(share_column[:], share_flipped[:, :chunks])
 
         with_labels = {}
-        for b in range(blocks // 2):
-            with_labels[b] = early.tile([P, BANK], F32, name=f"with_labels{b}")
-            nc.tensor.matmul(with_labels[b][:], identity[:], tables[b][:, :BANK], start=True, stop=False)
+        for lo in range(0, samples, BANK):
+            with_labels[lo] = early.tile([P, BANK], F32, name=f"with_labels{lo}")
+            nc.tensor.matmul(with_labels[lo][:], identity[:], tables[0][:, lo : lo + BANK], start=True, stop=False)
 
         def negate(b):
             minus_table = work.tile([P, samples], F32, name="minus_table")
@@ -89,9 +89,9 @@ def tile_cutmix_kernel(tc, labels, lam, dec, offs, out):
                 for at in range(0, BANK, P):
                     r = (lo + at) // P
                     nc.scalar.mul(step_flipped[:, lo + at : lo + at + P], flipped[:, at : at + P], share_column[:, r : r + 1])
-                on_labels = lo == 0 and b in with_labels
+                on_labels = b == 0
                 if on_labels:
-                    summed = with_labels[b]
+                    summed = with_labels[lo]
                 else:
                     summed = wait.tile([P, BANK], F32, name="step")
                 for at in range(0, BANK, P):

@@ -21,7 +21,7 @@ def tile_cutmix_kernel(tc, labels, lam, dec, offs, out):
         tc.tile_pool(name="work", bufs=4) as work,
         tc.psum_pool(name="early", bufs=1) as early,
         tc.psum_pool(name="turn", bufs=2) as turn,
-        tc.psum_pool(name="wait", bufs=4) as wait,
+        tc.psum_pool(name="wait", bufs=3) as wait,
     ):
         offsets = held.tile([P, samples // 16], U16, name="offsets")
         nc.sync.dma_start(offsets[:], offs)
@@ -52,9 +52,9 @@ def tile_cutmix_kernel(tc, labels, lam, dec, offs, out):
         nc.scalar.copy(share_column[:], share_flipped[:, :chunks])
 
         with_labels = {}
-        for lo in range(0, samples, BANK):
-            with_labels[lo] = early.tile([P, BANK], F32, name=f"with_labels{lo}")
-            nc.tensor.matmul(with_labels[lo][:], identity[:], tables[0][:, lo : lo + BANK], start=True, stop=False)
+        for b, lo in ((0, 0), (0, BANK), (1, 0)):
+            with_labels[b, lo] = early.tile([P, BANK], F32, name=f"with_labels{b}_{lo}")
+            nc.tensor.matmul(with_labels[b, lo][:], identity[:], tables[b][:, lo : lo + BANK], start=True, stop=False)
 
         def negate(b):
             minus_table = work.tile([P, samples], F32, name="minus_table")
@@ -89,9 +89,9 @@ def tile_cutmix_kernel(tc, labels, lam, dec, offs, out):
                 for at in range(0, BANK, P):
                     r = (lo + at) // P
                     nc.scalar.mul(step_flipped[:, lo + at : lo + at + P], flipped[:, at : at + P], share_column[:, r : r + 1])
-                on_labels = b == 0
+                on_labels = (b, lo) in with_labels
                 if on_labels:
-                    summed = with_labels[lo]
+                    summed = with_labels[b, lo]
                 else:
                     summed = wait.tile([P, BANK], F32, name="step")
                 for at in range(0, BANK, P):

import concourse.mybir as mybir
from concourse.masks import make_identity

F32 = mybir.dt.float32
U16 = mybir.dt.uint16
MULT = mybir.AluOpType.mult
ADD = mybir.AluOpType.add

P = 128
BANK = 512


def tile_cutmix_kernel(tc, labels, lam, dec, offs, out):
    nc = tc.nc
    classes, samples = labels.shape
    blocks = classes // P
    chunks = samples // P

    with (
        tc.tile_pool(name="held", bufs=1) as held,
        tc.tile_pool(name="work", bufs=4) as work,
        tc.psum_pool(name="early", bufs=1) as early,
        tc.psum_pool(name="turn", bufs=2) as turn,
        tc.psum_pool(name="wait", bufs=3) as wait,
    ):
        offsets = held.tile([P, samples // 16], U16, name="offsets")
        nc.sync.dma_start(offsets[:], offs)

        lam_folded = held.tile([chunks, P], F32, name="lam_folded")
        dec_folded = held.tile([chunks, P], F32, name="dec_folded")
        nc.sync.dma_start(lam_folded[:], lam[0, :].rearrange("(r n) -> r n", r=chunks))
        nc.sync.dma_start(dec_folded[:], dec[0, :].rearrange("(r n) -> r n", r=chunks))

        tables = []
        for b in range(blocks):
            table = held.tile([P, samples], F32, name=f"table{b}")
            width = samples // 2 if b == 0 else samples
            for lo in range(0, samples, width):
                nc.sync.dma_start(table[:, lo : lo + width], labels[b * P : (b + 1) * P, lo : lo + width])
            tables.append(table)

        identity = held.tile([P, P], F32, name="identity")
        make_identity(nc, identity[:])

        share_folded = held.tile([P, P], F32, name="share_folded")
        nc.gpsimd.memset(share_folded[:], 0.0)
        nc.vector.tensor_scalar(share_folded[:chunks, :], lam_folded[:], -1.0, 1.0, MULT, ADD)
        nc.vector.tensor_tensor(share_folded[:chunks, :], share_folded[:chunks, :], dec_folded[:], MULT)
        share_flipped = turn.tile([P, BANK], F32, name="flipped")
        nc.tensor.transpose(share_flipped[:, :P], share_folded[:], identity[:])
        share_column = held.tile([P, chunks], F32, name="share_column")
        nc.scalar.copy(share_column[:], share_flipped[:, :chunks])

        with_labels = {}
        for b, lo in ((0, 0), (0, BANK), (1, 0)):
            with_labels[b, lo] = early.tile([P, BANK], F32, name=f"with_labels{b}_{lo}")
            nc.tensor.matmul(with_labels[b, lo][:], identity[:], tables[b][:, lo : lo + BANK], start=True, stop=False)

        def negate(b):
            minus_table = work.tile([P, samples], F32, name="minus_table")
            width = samples // 2 if b == 0 else samples
            for lo in range(0, samples, width):
                nc.scalar.mul(minus_table[:, lo : lo + width], tables[b][:, lo : lo + width], -1.0)
            return minus_table

        minus_ahead = negate(0)
        for b in range(blocks):
            rows = slice(b * P, (b + 1) * P)
            table = tables[b]
            minus_table = minus_ahead
            if b + 1 < blocks:
                minus_ahead = negate(b + 1)

            away = work.tile([P, samples], F32, name="away")
            width = samples // 2 if b in (0, blocks - 1) else samples
            for lo in range(0, samples, width):
                hi = lo + width
                nc.vector.tensor_tensor(
                    away[:, lo:hi], table[:].indirect(offsets[:, lo // 16 : hi // 16]), minus_table[:, lo:hi], ADD
                )

            step_flipped = work.tile([P, samples], F32, name="step_flipped")
            mixed = work.tile([P, samples], F32, name="mixed")
            for lo in range(0, samples, BANK):
                hi = lo + BANK
                flipped = turn.tile([P, BANK], F32, name="flipped")
                for at in range(0, BANK, P):
                    nc.tensor.transpose(flipped[:, at : at + P], away[:, lo + at : lo + at + P], identity[:])
                for at in range(0, BANK, P):
                    r = (lo + at) // P
                    nc.scalar.mul(step_flipped[:, lo + at : lo + at + P], flipped[:, at : at + P], share_column[:, r : r + 1])
                on_labels = (b, lo) in with_labels
                if on_labels:
                    summed = with_labels[b, lo]
                else:
                    summed = wait.tile([P, BANK], F32, name="step")
                for at in range(0, BANK, P):
                    nc.tensor.matmul(
                        summed[:, at : at + P],
                        step_flipped[:, lo + at : lo + at + P],
                        identity[:],
                        is_transpose=True,
                        start=(at == 0 and not on_labels),
                        stop=(at == BANK - P),
                    )
                if on_labels:
                    nc.scalar.copy(mixed[:, lo:hi], summed[:])
                    nc.sync.dma_start(out[rows, lo:hi], mixed[:, lo:hi])
                else:
                    nc.vector.tensor_tensor(mixed[:, lo:hi], summed[:], table[:, lo:hi], ADD)
                    nc.sync.dma_start(out[rows, lo:hi], mixed[:, lo:hi])
